import numpy as np
import ml_dtypes


def mxq(x, axis, fmt="e4m3"):
    dtype, down = {"e4m3": (ml_dtypes.float8_e4m3fn, 7), "e5m2": (ml_dtypes.float8_e5m2, 14)}[fmt]
    v = np.moveaxis(np.asarray(x, np.float32).astype(ml_dtypes.bfloat16).astype(np.float64), axis, -1)
    blocks = v.reshape(v.shape[:-1] + (-1, 32))
    amax = np.abs(blocks).max(-1, keepdims=True)
    byte = np.maximum(np.where(amax > 0, np.frexp(amax)[1] - 1 + 127, 0) - down, 1)
    scale = np.exp2(byte - 127.0)
    codes = (blocks / scale).astype(np.float32).astype(dtype).astype(np.float64)
    return np.moveaxis((codes * scale).reshape(v.shape), -1, axis)


WIDE = False


def mx_kscale(k):
    if not WIDE:
        return np.ones(k)
    levels = np.array([10, -10, 5, -5, 0])
    if k % 512:
        return np.exp2(np.random.permutation(np.resize(levels, k // 32))).repeat(32)
    a = np.empty((k // 512, 16))
    for p in range(k // 512):
        a[p, :8] = np.random.permutation(np.resize(levels, 8))
        for g in range(8):
            far = levels[np.abs(levels - a[p, g]) >= 10]
            a[p, g + 8] = far[np.random.randint(len(far))]
    return np.exp2(a.ravel()).repeat(32)


BF16 = ml_dtypes.bfloat16


def bf(x):
    return np.asarray(x, np.float32).astype(BF16)


def f64(x):
    return np.asarray(x).astype(np.float64)


B, C, HH, WW = 4, 512, 32, 32
P = HH * WW


def sigmoid(v):
    return 1.0 / (1.0 + np.exp(-v))


def draw0():
    s2, s3, t = mx_kscale(C), mx_kscale(C), mx_kscale(C)
    lev = np.random.uniform(0.5, 1.5, (B, C, 1, 1))
    x = (lev + 0.8 * np.random.standard_normal((B, C, HH, WW))) * t[None, :, None, None]
    return {"x": bf(x),
            "wh_in": bf(np.random.standard_normal((B, C, HH, WW)) * 1.1 * s2[None, :, None, None]),
            "gray_in": bf(np.random.standard_normal((B, C, HH, WW)) * 0.6 * s3[None, :, None, None]),
            "W2": bf(np.random.standard_normal((C, C)) * 1.3 / np.sqrt(C) / s2[None, :]), "b2": bf(np.random.standard_normal(C) * 0.5),
            "W3": bf(np.random.standard_normal((C, C)) * 2.5 / np.sqrt(C) / s3[None, :]), "b3": bf(np.random.standard_normal(C) * 0.5),
            "W4": bf(np.random.standard_normal((C, C)) * 0.5 / np.sqrt(C) / t[None, :]), "b4": bf(np.random.standard_normal(C) * 0.5)}


def core(x, wh_in, gray_in, W2, b2, W3, b3, W4, b4):
    wh = (mxq(f64(W2), 1, "e4m3") @ mxq(f64(wh_in), 1, "e4m3").reshape(B, C, P)) + f64(b2)[None, :, None]
    wh_weight = sigmoid(np.tanh(wh))
    gray = (mxq(f64(W3), 1, "e4m3") @ mxq(f64(gray_in), 1, "e4m3").reshape(B, C, P)) + f64(b3)[None, :, None]
    gray_weight = sigmoid(np.tanh(gray))
    h = f64(x).reshape(B, C, P) * (1.0 + wh_weight + gray_weight)
    out = (mxq(f64(W4), 1, "e4m3") @ mxq(h, 1, "e4m3")) + f64(b4)[None, :, None]
    return out.reshape(B, C, HH, WW)


def e4m3fn_bytes(y):
    return np.clip(np.asarray(y, np.float64), -448.0, 448.0).astype(np.float32).astype(ml_dtypes.float8_e4m3fn).view(np.uint8)


def e4m3fn_values(b):
    return np.asarray(b, np.uint8).view(ml_dtypes.float8_e4m3fn).astype(np.float64)


def setup_inputs():
    d = draw0()
    x0 = np.asarray(d['wh_in']).astype(np.float64)
    s = (np.max(np.abs(x0), axis=(0, 2, 3), keepdims=True) / 448.0).astype(np.float32)
    out = {}
    for k, v in d.items():
        if k == 'wh_in':
            out['wh_in_bytes'] = e4m3fn_bytes(x0 / s.astype(np.float64))
            out['wh_in_scale'] = s
        else:
            out[k] = v
    return out


def reference(x, wh_in_bytes, wh_in_scale, gray_in, W2, b2, W3, b3, W4, b4):
    return core(x, e4m3fn_values(wh_in_bytes) * wh_in_scale.astype(np.float64), gray_in, W2, b2, W3, b3, W4, b4)

@@ -1,0 +1,340 @@
+from contextlib import ExitStack
+
+import concourse.mybir as mybir
+from concourse.masks import make_identity
+
+B, C, P_IMG = 4, 512, 1024
+P = 128
+J = 4
+FLOPS = 3 * 2 * B * C * C * P_IMG
+
+F32 = mybir.dt.float32
+BF16 = mybir.dt.bfloat16
+U32 = mybir.dt.uint32
+U8 = mybir.dt.uint8
+FP8 = mybir.dt.float8_e4m3fn
+FP8X4 = mybir.dt.float8_e4m3fn_x4
+ALU = mybir.AluOpType
+ACT = mybir.ActivationFunctionType
+
+LOADS = [(0, 0, 256), (0, 256, 256), (0, 512, 512), (1, 0, 1024), (2, 0, 1024), (3, 0, 1024)]
+LOAD_ORDER = "W30 W20 g0 w0 W31 W21 W40 g1 w1 W41 w2 g2 x2 x0 g3 x1 g5 w3 x3 g4 w4 x4 w5 x5"
+SPLIT_STORES = 1
+CHUNKS = [
+    (0, 0, 256), (0, 256, 256), (0, 512, 512),
+    (1, 0, 512), (1, 512, 512),
+    (2, 0, 512), (2, 512, 512),
+    (3, 0, 512), (3, 512, 256), (3, 768, 256),
+]
+OUT_ON_VECTOR = [[0,1],[],[0,1,2],[0],[0,1],[0,1],[],[0,1,2],[],[0]]
+A_BUFS, O_BUFS, S_BUFS = 4, 4, 0
+SLAB = 128
+PE_SLABS = {128: 0, 256: 0, 512: 0}
+HEAD = [("gil", 0),("ww", 0),("wt", "30"),("gq", 0),("wt", "20"),("wil", 0),("wq", 0),("wt", "31"),("wt", "21"),("wcs", "30"),("wqz", "30"),("wcs", "20"),("wt", "40"),("wcs", "31"),("wcs", "21"),("wqz", "20"),("wqz", "31"),("ww", 1),("wcs", "40"),("m1g", 0),("wqz", "40"),("gil", 1),("wil", 1),("wt", "41"),("t1g", 0),("wqz", "21"),("wq", 1),("gil", 2),("wcs", "41"),("wqz", "41")]
+ORDER = [("m1g", 1),("ev", -1),("t2b", 0),("ww", 2),("es", -1),("sum", 0),("t2a", 0),("gil", 2),("psum", 0),("mulp", 0),("t1g", 1),("m1w", 1),("mul", 0),("hq", 0),("wil", 2),("t1w", 1),("gq", 2),("m2", 0),("wq", 2)]
+
+
+def tile_wb_pb_t_kernel(tc, x, wh_bytes, wh_scale, gray, W2, b2, W3, b3, W4, b4, out):
+    nc = tc.nc
+    n_chunks = len(CHUNKS)
+
+    with ExitStack() as ctx:
+        keep = ctx.enter_context(tc.tile_pool(name="keep", bufs=1))
+        work = ctx.enter_context(tc.tile_pool(name="work", bufs=2))
+        psum = ctx.enter_context(tc.psum_pool(name="psum", bufs=4))
+
+        ident = keep.tile([P, P], F32, name="ident", align_bytes=64)
+        make_identity(nc, ident[:])
+        ctx.enter_context(tc.manual_schedule())
+
+        warm = keep.tile([P, 1], F32, name="warm")
+        nc.vector.memset(warm[:], 0.0)
+        nc.scalar.activation(out=warm[:], in_=warm[:], func=ACT.Tanh)
+
+        w_rows = {}
+        bias_b = {}
+        imgs = {}
+
+        def load_w(nm, w, h):
+            if h == 0:
+                w_rows[nm] = keep.tile([P, J, C], BF16, name="wrows_" + nm, align_bytes=64)
+            src = w.rearrange("(m t) k -> m t k", t=J)
+            nc.sync.dma_start(out=w_rows[nm][:, 2 * h : 2 * h + 2, :], in_=src[:, 2 * h : 2 * h + 2, :])
+
+        def load_bias(nm, b):
+            t = keep.tile([P, J], BF16, name="biasb_" + nm)
+            nc.scalar.dma_start(out=t[:], in_=b.rearrange("(p t) -> p t", t=J))
+            bias_b[nm] = t
+
+        def load_img(nm, src, u, dt):
+            b, c0, n = LOADS[u]
+            t = keep.tile([P, J, n], dt, name="%s_%d" % (nm, u), align_bytes=64)
+            v = src[b].rearrange("(p t) h w -> p t (h w)", t=J)
+            nc.sync.dma_start(out=t[:], in_=v[:, :, c0 : c0 + n])
+            imgs[(nm, u)] = t
+
+        def find(nm, c):
+            b, c0, n = CHUNKS[c]
+            for u in range(len(LOADS)):
+                lb, l0, ln = LOADS[u]
+                if lb == b and l0 <= c0 and c0 + n <= l0 + ln:
+                    return imgs[(nm, u)], c0 - l0, n
+            return None
+
+        scale = keep.tile([P, J], F32, name="scale")
+        nc.scalar.dma_start(out=scale[:], in_=wh_scale.rearrange("o (p t) a b -> p (o t a b)", t=J))
+        load_bias("3", b3)
+        load_bias("2", b2)
+        load_bias("4", b4)
+        srcs = {"g": ("gray", gray, BF16), "w": ("wh", wh_bytes, U8), "x": ("x", x, BF16)}
+        for item in LOAD_ORDER.split():
+            if item[0] == "W":
+                load_w(item[1], {"2": W2, "3": W3, "4": W4}[item[1]], int(item[2]))
+            else:
+                nm, src, dt = srcs[item[0]]
+                load_img(nm, src, int(item[1:]), dt)
+
+        w_codes, w_scales, w_grp, w_ps = {}, {}, {}, {}
+
+        def w_transpose(nm, h):
+            ps = psum.tile([P, 2, 2, P], F32, name="wps_%s%d" % (nm, h), tag="o", bufs=O_BUFS)
+            for s in range(2):
+                words = w_rows[nm][:, 2 * h + s, :].bitcast(F32)
+                for u in range(2):
+                    nc.tensor.transpose(ps[:, s, u, :], words[:, u : C // 2 : 2], ident[:])
+            w_ps[(nm, h)] = ps
+            if h == 0:
+                w_grp[nm] = keep.tile([P, C * J], BF16, name="wgrp_" + nm, align_bytes=64)
+
+        def w_copy(nm, h, eng):
+            dst = w_grp[nm][:].bitcast(F32).rearrange("p (h s m u) -> p h s m u", h=2, s=2, u=2)[:, h]
+            src = w_ps[(nm, h)][:].rearrange("p s u m -> p s m u")
+            if eng == "v":
+                nc.vector.tensor_copy(out=dst, in_=src)
+            else:
+                nc.scalar.copy(out=dst, in_=src)
+
+        def w_quant(nm, h):
+            if h == 0:
+                w_codes[nm] = keep.tile([P, C], U32, name="wcodes_" + nm, align_bytes=64)
+                w_scales[nm] = keep.tile([P, C], U8, name="wscales_" + nm, align_bytes=64)
+            cols = slice(C // 2 * h, C // 2 * (h + 1))
+            nc.vector.quantize_mx(
+                out=w_codes[nm][:, cols].bitcast(FP8X4), scales=w_scales[nm][:, cols],
+                in_=w_grp[nm][:, C // 2 * J * h : C // 2 * J * (h + 1)])
+
+        bias = {}
+
+        def bias_cast(nm):
+            bias[nm] = keep.tile([P, J], F32, name="bias_" + nm)
+            nc.vector.tensor_copy(out=bias[nm][:], in_=bias_b[nm][:])
+
+        st = {}
+
+        def quant(nm, c, grp, n):
+            codes = work.tile([P, n], U32, name="codes_%s_%d" % (nm, c), tag="codes_" + nm, align_bytes=64)
+            scs = work.tile([P, n], U8, name="scs_%s_%d" % (nm, c), tag="scs_" + nm, align_bytes=64)
+            nc.vector.quantize_mx(out=codes[:].bitcast(FP8X4), scales=scs[:], in_=grp[:].rearrange("p n t -> p (n t)"))
+            st[(nm, c)] = (codes, scs)
+
+        def gray_il(c):
+            t, off, n = find("gray", c)
+            g = work.tile([P, n, J], BF16, name="ggrp_%d" % c, tag="ggrp", align_bytes=64)
+            nc.vector.tensor_copy(
+                out=g[:].rearrange("p (c i) t -> p c t i", i=4),
+                in_=t[:, :, off : off + n].rearrange("p t (c i) -> p c t i", i=4),
+            )
+            st[("ggrp", c)] = g
+
+        def gray_q(c):
+            quant("g", c, st[("ggrp", c)], CHUNKS[c][2])
+
+        def wh_widen(c):
+            t, off, n = find("wh", c)
+            wd = work.tile([P, J, n], BF16, name="wide_%d" % c, tag="wide", align_bytes=64)
+            for j in range(J):
+                nc.vector.tensor_scalar(
+                    out=wd[:, j, :], in0=t[:, j, off : off + n].bitcast(FP8),
+                    scalar1=scale[:, j : j + 1], scalar2=None, op0=ALU.mult,
+                )
+            st[("wide", c)] = wd
+
+        def wh_il(c):
+            n = CHUNKS[c][2]
+            g = work.tile([P, n, J], BF16, name="wgrp_%d" % c, tag="wgrp", align_bytes=64)
+            nc.vector.tensor_copy(
+                out=g[:].rearrange("p (c i) t -> p c t i", i=4),
+                in_=st[("wide", c)][:].rearrange("p t (c i) -> p c t i", i=4),
+            )
+            st[("whgrp", c)] = g
+
+        def wh_q(c):
+            quant("w", c, st[("whgrp", c)], CHUNKS[c][2])
+
+        def product(nm, wn, c, tag, j):
+            n = CHUNKS[c][2]
+            codes, scs = st[(nm, c)]
+            ps = psum.tile([P, n], F32, name="ps_%s_%d_%d" % (nm, c, j), tag=tag, bufs=A_BUFS if tag == "a" else O_BUFS)
+            cols = slice(P * j, P * (j + 1))
+            nc.tensor.matmul_mx(
+                out=ps[:], lhsT=w_codes[wn][:, cols].bitcast(FP8X4), lhsT_scale=w_scales[wn][:, cols],
+                rhs=codes[:].bitcast(FP8X4), rhs_scale=scs[:], start=True, stop=True,
+            )
+            st[("ps" + nm, c, j)] = ps
+
+        def gate_in(nm, wn, c):
+            for j in range(J):
+                product(nm, wn, c, "a", j)
+
+        def tanh_in(nm, wn, c):
+            n = CHUNKS[c][2]
+            if ("t", c) not in st:
+                st[("t", c)] = work.tile([P, 2, J, n], F32, name="t_%d" % c, tag="t", align_bytes=64)
+            t = st[("t", c)]
+            k = 0 if nm == "g" else 1
+            for j in range(J):
+                nc.scalar.activation(out=t[:, k, j, :], in_=st[("ps" + nm, c, j)][:], func=ACT.Tanh, bias=bias[wn][:, j : j + 1])
+
+        def tanh_out(c, lo, hi):
+            if lo == hi:
+                return
+            part = st[("t", c)][:, :, :, lo:hi]
+            nc.scalar.activation(out=part, in_=part, func=ACT.Tanh, scale=0.5)
+
+        def split(c):
+            n = CHUNKS[c][2]
+            return n, PE_SLABS[n] * SLAB
+
+        def pe_sum(c):
+            n, m = split(c)
+            for lo in range(0, m, SLAB):
+                ps = psum.tile([P, J, SLAB], F32, name="gs_%d_%d" % (c, lo), tag="s", bufs=S_BUFS)
+                for k in range(2):
+                    nc.tensor.matmul(out=ps[:], lhsT=ident[:], rhs=st[("t", c)][:, k, :, lo : lo + SLAB], start=(k == 0), stop=(k == 1))
+                st[("gs", c, lo)] = ps
+
+        def get_h(c):
+            if ("hgrp", c) not in st:
+                st[("hgrp", c)] = work.tile([P, CHUNKS[c][2], J], BF16, name="h_%d" % c, tag="h", align_bytes=64)
+            return st[("hgrp", c)]
+
+        def pe_mul(c):
+            n, m = split(c)
+            xt, off, n = find("x", c)
+            h = get_h(c)
+            for lo in range(0, m, SLAB):
+                nc.vector.scalar_tensor_tensor(
+                    out=h[:, lo : lo + SLAB, :], in0=st[("gs", c, lo)][:].rearrange("p t n -> p n t"), scalar=4.0,
+                    in1=xt[:, :, off + lo : off + lo + SLAB].rearrange("p t n -> p n t"), op0=ALU.add, op1=ALU.mult,
+                )
+
+        def gate_sum(c):
+            n, m = split(c)
+            if m == n:
+                return
+            t = st[("t", c)]
+            nc.vector.scalar_tensor_tensor(
+                out=t[:, 0, :, m:n], in0=t[:, 1, :, m:n], scalar=4.0, in1=t[:, 0, :, m:n], op0=ALU.add, op1=ALU.add)
+
+        def gate_mul(c):
+            n, m = split(c)
+            if m == n:
+                return
+            xt, off, n = find("x", c)
+            h = get_h(c)
+            nc.vector.tensor_tensor(
+                out=h[:, m:n, :].rearrange("p (c i) t -> p c t i", i=4),
+                in0=st[("t", c)][:, 0, :, m:n].rearrange("p t (c i) -> p c t i", i=4),
+                in1=xt[:, :, off + m : off + n].rearrange("p t (c i) -> p c t i", i=4),
+                op=ALU.mult,
+            )
+
+        def h_q(c):
+            quant("h", c, st[("hgrp", c)], CHUNKS[c][2])
+
+        def conv_out(c):
+            n = CHUNKS[c][2]
+            for j in range(J):
+                product("h", "4", c, "o", j)
+            st[("o", c)] = work.tile([P, J, n], F32, name="o_%d" % c, tag="o", align_bytes=64)
+
+        def empty_v(c):
+            for j in OUT_ON_VECTOR[c]:
+                nc.vector.tensor_scalar(
+                    out=st[("o", c)][:, j, :], in0=st[("psh", c, j)][:], scalar1=0.5, scalar2=bias["4"][:, j : j + 1],
+                    op0=ALU.mult, op1=ALU.add,
+                )
+
+        def empty_s(c):
+            for j in range(J):
+                if j not in OUT_ON_VECTOR[c]:
+                    nc.scalar.activation(
+                        out=st[("o", c)][:, j, :], in_=st[("psh", c, j)][:], func=ACT.Identity, scale=0.5, bias=bias["4"][:, j : j + 1],
+                    )
+
+        def store(c):
+            b, c0, n = CHUNKS[c]
+            v = out[b].rearrange("(p t) h w -> p t (h w)", t=J)
+            step = 2 if c >= n_chunks - SPLIT_STORES else J
+            for j in range(0, J, step):
+                nc.sync.dma_start(out=v[:, j : j + step, c0 : c0 + n], in_=st[("o", c)][:, j : j + step, :])
+
+        def emit(task, c):
+            if task == "wt":
+                w_transpose(c[0], int(c[1]))
+            elif task in ("wcs", "wcv"):
+                w_copy(c[0], int(c[1]), task[2])
+            elif task == "wqz":
+                if c[1] == "0":
+                    bias_cast(c[0])
+                w_quant(c[0], int(c[1]))
+            elif task == "gil":
+                gray_il(c)
+            elif task == "gq":
+                gray_q(c)
+            elif task == "ww":
+                wh_widen(c)
+            elif task == "wil":
+                wh_il(c)
+            elif task == "wq":
+                wh_q(c)
+            elif task == "m1g":
+                gate_in("g", "3", c)
+            elif task == "m1w":
+                gate_in("w", "2", c)
+            elif task == "t1g":
+                tanh_in("g", "3", c)
+            elif task == "t1w":
+                tanh_in("w", "2", c)
+            elif task == "t2a":
+                tanh_out(c, 0, split(c)[1])
+            elif task == "t2b":
+                tanh_out(c, *split(c)[::-1])
+            elif task == "psum":
+                pe_sum(c)
+            elif task == "mulp":
+                pe_mul(c)
+            elif task == "sum":
+                gate_sum(c)
+            elif task == "mul":
+                gate_mul(c)
+            elif task == "hq":
+                h_q(c)
+            elif task == "m2":
+                conv_out(c)
+            elif task == "ev":
+                empty_v(c)
+            elif task == "es":
+                empty_s(c)
+                store(c)
+
+        done = set()
+        for task, c in HEAD:
+            emit(task, c)
+            done.add((task, c))
+        for i in range(-3, n_chunks + 4):
+            for task, off in ORDER:
+                c = i + off
+                if 0 <= c < n_chunks and (task, c) not in done:
+                    emit(task, c)
+                    done.add((task, c))

@@ -18,20 +18,20 @@ ALU = mybir.AluOpType
 ACT = mybir.ActivationFunctionType
 
 LOADS = [(0, 0, 256), (0, 256, 256), (0, 512, 512), (1, 0, 1024), (2, 0, 1024), (3, 0, 1024)]
-LOAD_ORDER = "W30 W20 g0 w0 W31 W21 W40 g1 w1 W41 w2 g2 x2 x0 g3 x1 g5 w3 x3 g4 w4 x4 w5 x5"
+LOAD_ORDER = "W30 g0 W20 w0 W31 W21 W40 g1 w1 W41 w2 g2 g5 x0 w4 w3 x2 g3 x1 x3 g4 x4 w5 x5"
 SPLIT_STORES = 1
 CHUNKS = [
     (0, 0, 256), (0, 256, 256), (0, 512, 512),
     (1, 0, 512), (1, 512, 512),
     (2, 0, 512), (2, 512, 512),
-    (3, 0, 512), (3, 512, 256), (3, 768, 256),
+    (3, 0, 512), (3, 512, 256), (3, 768, 128), (3, 896, 128),
 ]
-OUT_ON_VECTOR = [[0,1],[],[0,1,2],[0],[0,1],[0,1],[],[0,1,2],[],[0]]
+OUT_ON_VECTOR = [[0],[0,1],[],[0],[0,1],[0,1,2],[0],[],[0,1,2],[0,1,2],[0]]
 A_BUFS, O_BUFS, S_BUFS = 4, 4, 0
 SLAB = 128
 PE_SLABS = {128: 0, 256: 0, 512: 0}
-HEAD = [("gil", 0),("ww", 0),("wt", "30"),("gq", 0),("wt", "20"),("wil", 0),("wq", 0),("wt", "31"),("wt", "21"),("wcs", "30"),("wqz", "30"),("wcs", "20"),("wt", "40"),("wcs", "31"),("wcs", "21"),("wqz", "20"),("wqz", "31"),("ww", 1),("wcs", "40"),("m1g", 0),("wqz", "40"),("gil", 1),("wil", 1),("wt", "41"),("t1g", 0),("wqz", "21"),("wq", 1),("gil", 2),("wcs", "41"),("wqz", "41")]
-ORDER = [("m1g", 1),("ev", -1),("t2b", 0),("ww", 2),("es", -1),("sum", 0),("t2a", 0),("gil", 2),("psum", 0),("mulp", 0),("t1g", 1),("m1w", 1),("mul", 0),("hq", 0),("wil", 2),("t1w", 1),("gq", 2),("m2", 0),("wq", 2)]
+HEAD = [("wt", "30"),("gil", 0),("wcs", "30"),("wt", "20"),("gq", 0),("ww", 0),("wcs", "20"),("wt", "31"),("wt", "21"),("wqz", "30"),("wcs", "31"),("wqz", "20"),("wil", 0),("wqz", "31"),("wcs", "21"),("wq", 0),("wt", "40"),("gil", 1),("ww", 1),("m1g", 0),("wil", 1),("wqz", "21"),("wcs", "40"),("wqz", "40"),("wt", "41"),("wq", 1),("t1g", 0),("gil", 2),("wcs", "41"),("m1w", 0),("wqz", "41")]
+ORDER = [("ww", 2),("t2a", 0),("t2b", 0),("psum", 0),("m1g", 1),("ev", -1),("es", -1),("sum", 0),("mulp", 0),("wil", 2),("mul", 0),("t1g", 1),("gil", 2),("hq", 0),("m1w", 1),("wq", 2),("gq", 2),("t1w", 1),("m2", 0)]
 
 
 def tile_wb_pb_t_kernel(tc, x, wh_bytes, wh_scale, gray, W2, b2, W3, b3, W4, b4, out):

@@ -18,20 +18,13 @@ ALU = mybir.AluOpType
 ACT = mybir.ActivationFunctionType
 
 LOADS = [(0, 0, 256), (0, 256, 256), (0, 512, 512), (1, 0, 1024), (2, 0, 1024), (3, 0, 1024)]
-LOAD_ORDER = "W30 g0 W20 w0 W31 W21 W40 g1 w1 W41 w2 g2 g5 x0 w4 w3 x2 g3 x1 x3 g4 x4 w5 x5"
-SPLIT_STORES = 1
-CHUNKS = [
-    (0, 0, 256), (0, 256, 256), (0, 512, 512),
-    (1, 0, 512), (1, 512, 512),
-    (2, 0, 512), (2, 512, 512),
-    (3, 0, 512), (3, 512, 256), (3, 768, 128), (3, 896, 128),
-]
-OUT_ON_VECTOR = [[0],[0,1],[],[0],[0,1],[0,1,2],[0],[],[0,1,2],[0,1,2],[0]]
-A_BUFS, O_BUFS, S_BUFS = 4, 4, 0
+LOAD_ORDER = "w0 w1 W20 W21 w2 g0 W30 W31 g1 w3 g2 W40 x0 W41 g4 g3 x1 g5 w5 x4 w4 x3 x2 x5"
+CHUNKS = [(0, 0, 256), (0, 256, 256), (0, 512, 512), (1, 0, 512), (1, 512, 512), (2, 0, 512), (2, 512, 512), (3, 0, 512), (3, 512, 256), (3, 768, 256)]
+A_BUFS = 8
 SLAB = 128
-PE_SLABS = {128: 0, 256: 0, 512: 0}
-HEAD = [("wt", "30"),("gil", 0),("wcs", "30"),("wt", "20"),("gq", 0),("ww", 0),("wcs", "20"),("wt", "31"),("wt", "21"),("wqz", "30"),("wcs", "31"),("wqz", "20"),("wil", 0),("wqz", "31"),("wcs", "21"),("wq", 0),("wt", "40"),("gil", 1),("ww", 1),("m1g", 0),("wil", 1),("wqz", "21"),("wcs", "40"),("wqz", "40"),("wt", "41"),("wq", 1),("t1g", 0),("gil", 2),("wcs", "41"),("m1w", 0),("wqz", "41")]
-ORDER = [("ww", 2),("t2a", 0),("t2b", 0),("psum", 0),("m1g", 1),("ev", -1),("es", -1),("sum", 0),("mulp", 0),("wil", 2),("mul", 0),("t1g", 1),("gil", 2),("hq", 0),("m1w", 1),("wq", 2),("gq", 2),("t1w", 1),("m2", 0)]
+FRONT_BUFS = 1
+PE_CHUNKS = ()
+SEQ = "wt:20 wws:1 wcs:20 wt:21 wwv:0 wil:0 wq:0 wil:1 wqz:20 wcs:21 wq:1 wqz:21 gis:0 mw:0 wt:30 wwv:2 gq:0 wt:31 tw:0 wil:2 giv:1 wcs:30 wcs:31 wqz:30 wqz:31 gq:1 mw:1 tw:1 mg:0 tg:0 wwv:3 giv:2 wq:2 ub:0 sum:0 gq:2 mul:0 mg:1 wt:40 wil:3 tg:1 giv:3 wcs:40 mg:2 wq:3 mw:2 ub:1 tg:2 hq:0 tw:2 wt:41 gq:3 sum:1 mw:3 wqz:40 mul:1 wcs:41 ma:0 ub:2 wqz:41 tw:3 mb:0 giv:4 mg:3 es:0.3 sum:2 hq:1 tg:3 ev:0.0 mul:2 ev:0.1 es:0.2 wwv:4 mw:4 hq:2 ub:3 gq:4 tw:4 sum:3 wil:4 ma:2 mg:4 mb:2 ev:2.2 es:2.1 tg:4 st:0.0.4 es:2.3 mul:3 wq:4 es:2.0 giv:5 ub:4 sum:4 mg:5 mb:1 gq:5 tg:5 mw:5 tw:5 ma:1 hq:3 es:1.2 mul:4 es:1.1 ub:5 ev:1.3 wwv:5 mg:6 tg:6 hq:4 ev:1.0 mw:6 tw:6 mb:4 sum:5 st:2.0.4 es:4.3 wil:5 mg:7 mul:5 ev:4.2 ub:6 wq:5 mb:3 tg:7 mw:7 tw:7 sum:6 es:3.2 ev:3.3 ma:3 ev:3.0 ma:4 mul:6 ub:7 mw:8 ev:3.1 ev:4.0 tw:8 hq:5 ma:5 st:1.0.4 st:3.0.4 ev:4.1 st:4.0.4 mg:8 hq:6 tg:8 es:5.1 mb:5 sum:7 es:5.0 ev:5.2 mw:9 mul:7 ma:6 ub:8 tw:9 ev:5.3 ev:6.0 ev:6.1 mg:9 hq:7 mb:6 sum:8 mb:7 ev:6.3 tg:9 es:6.2 ma:7 ub:9 ev:7.2 ev:7.0 mul:8 sum:9 hq:8 st:5.0.4 mb:8 es:7.3 es:7.1 es:8.2 ma:8 mul:9 ev:8.0 es:8.3 hq:9 st:6.0.4 es:8.1 st:7.0.4 ma:9 mb:9 es:9.0 es:9.3 ev:9.1 st:8.0.4 st:9.0.2 ev:9.2 st:9.2.4"
 
 
 def tile_wb_pb_t_kernel(tc, x, wh_bytes, wh_scale, gray, W2, b2, W3, b3, W4, b4, out):
@@ -41,7 +34,7 @@ def tile_wb_pb_t_kernel(tc, x, wh_bytes, wh_scale, gray, W2, b2, W3, b3, W4, b4,
     with ExitStack() as ctx:
         keep = ctx.enter_context(tc.tile_pool(name="keep", bufs=1))
         work = ctx.enter_context(tc.tile_pool(name="work", bufs=2))
-        psum = ctx.enter_context(tc.psum_pool(name="psum", bufs=4))
+        psum = ctx.enter_context(tc.psum_pool(name="psum", bufs=8))
 
         ident = keep.tile([P, P], F32, name="ident", align_bytes=64)
         make_identity(nc, ident[:])
@@ -56,7 +49,7 @@ def tile_wb_pb_t_kernel(tc, x, wh_bytes, wh_scale, gray, W2, b2, W3, b3, W4, b4,
         imgs = {}
 
         def load_w(nm, w, h):
-            if h == 0:
+            if nm not in w_rows:
                 w_rows[nm] = keep.tile([P, J, C], BF16, name="wrows_" + nm, align_bytes=64)
             src = w.rearrange("(m t) k -> m t k", t=J)
             nc.sync.dma_start(out=w_rows[nm][:, 2 * h : 2 * h + 2, :], in_=src[:, 2 * h : 2 * h + 2, :])
@@ -97,13 +90,13 @@ def tile_wb_pb_t_kernel(tc, x, wh_bytes, wh_scale, gray, W2, b2, W3, b3, W4, b4,
         w_codes, w_scales, w_grp, w_ps = {}, {}, {}, {}
 
         def w_transpose(nm, h):
-            ps = psum.tile([P, 2, 2, P], F32, name="wps_%s%d" % (nm, h), tag="o", bufs=O_BUFS)
+            ps = psum.tile([P, 2, 2, P], F32, name="wps_%s%d" % (nm, h), tag="a", bufs=A_BUFS)
             for s in range(2):
                 words = w_rows[nm][:, 2 * h + s, :].bitcast(F32)
                 for u in range(2):
                     nc.tensor.transpose(ps[:, s, u, :], words[:, u : C // 2 : 2], ident[:])
             w_ps[(nm, h)] = ps
-            if h == 0:
+            if nm not in w_grp:
                 w_grp[nm] = keep.tile([P, C * J], BF16, name="wgrp_" + nm, align_bytes=64)
 
         def w_copy(nm, h, eng):
@@ -115,7 +108,7 @@ def tile_wb_pb_t_kernel(tc, x, wh_bytes, wh_scale, gray, W2, b2, W3, b3, W4, b4,
                 nc.scalar.copy(out=dst, in_=src)
 
         def w_quant(nm, h):
-            if h == 0:
+            if nm not in w_codes:
                 w_codes[nm] = keep.tile([P, C], U32, name="wcodes_" + nm, align_bytes=64)
                 w_scales[nm] = keep.tile([P, C], U8, name="wscales_" + nm, align_bytes=64)
             cols = slice(C // 2 * h, C // 2 * (h + 1))
@@ -131,87 +124,94 @@ def tile_wb_pb_t_kernel(tc, x, wh_bytes, wh_scale, gray, W2, b2, W3, b3, W4, b4,
 
         st = {}
 
+        units = {}
+        for c in range(n_chunks):
+            b, c0, n = CHUNKS[c]
+            for u in range(len(LOADS)):
+                lb, l0, ln = LOADS[u]
+                if lb == b and l0 <= c0 and c0 + n <= l0 + ln:
+                    units[c] = (u, c0 - l0)
+
         def quant(nm, c, grp, n):
             codes = work.tile([P, n], U32, name="codes_%s_%d" % (nm, c), tag="codes_" + nm, align_bytes=64)
             scs = work.tile([P, n], U8, name="scs_%s_%d" % (nm, c), tag="scs_" + nm, align_bytes=64)
             nc.vector.quantize_mx(out=codes[:].bitcast(FP8X4), scales=scs[:], in_=grp[:].rearrange("p n t -> p (n t)"))
             st[(nm, c)] = (codes, scs)
 
-        def gray_il(c):
-            t, off, n = find("gray", c)
-            g = work.tile([P, n, J], BF16, name="ggrp_%d" % c, tag="ggrp", align_bytes=64)
-            nc.vector.tensor_copy(
-                out=g[:].rearrange("p (c i) t -> p c t i", i=4),
-                in_=t[:, :, off : off + n].rearrange("p t (c i) -> p c t i", i=4),
-            )
-            st[("ggrp", c)] = g
+        def gray_il(u, eng):
+            n = LOADS[u][2]
+            g = st.get(("ggrp", u)) or work.tile([P, n, J], BF16, name="ggrp_%d" % u, tag="ggrp", bufs=FRONT_BUFS, align_bytes=64)
+            dst = g[:].rearrange("p (c i) t -> p c t i", i=4)
+            src = imgs[("gray", u)][:].rearrange("p t (c i) -> p c t i", i=4)
+            if eng == "v":
+                nc.vector.tensor_copy(out=dst, in_=src)
+            else:
+                nc.scalar.copy(out=dst, in_=src)
+            st[("ggrp", u)] = g
 
-        def gray_q(c):
-            quant("g", c, st[("ggrp", c)], CHUNKS[c][2])
+        def gray_q(u):
+            quant("g", u, st[("ggrp", u)], LOADS[u][2])
 
-        def wh_widen(c):
-            t, off, n = find("wh", c)
-            wd = work.tile([P, J, n], BF16, name="wide_%d" % c, tag="wide", align_bytes=64)
+        def wh_widen(u, eng):
+            n = LOADS[u][2]
+            wd = st.get(("wide", u)) or work.tile([P, J, n], BF16, name="wide_%d" % u, tag="wide", bufs=2, align_bytes=64)
             for j in range(J):
-                nc.vector.tensor_scalar(
-                    out=wd[:, j, :], in0=t[:, j, off : off + n].bitcast(FP8),
-                    scalar1=scale[:, j : j + 1], scalar2=None, op0=ALU.mult,
-                )
-            st[("wide", c)] = wd
+                codes = imgs[("wh", u)][:, j, :].bitcast(FP8)
+                if eng == "v":
+                    nc.vector.tensor_scalar(out=wd[:, j, :], in0=codes, scalar1=scale[:, j : j + 1], scalar2=None, op0=ALU.mult)
+                else:
+                    nc.scalar.activation(out=wd[:, j, :], in_=codes, func=ACT.Copy, scale=scale[:, j : j + 1])
+            st[("wide", u)] = wd
 
-        def wh_il(c):
-            n = CHUNKS[c][2]
-            g = work.tile([P, n, J], BF16, name="wgrp_%d" % c, tag="wgrp", align_bytes=64)
+        def wh_il(u):
+            n = LOADS[u][2]
+            g = work.tile([P, n, J], BF16, name="wgrp_%d" % u, tag="wgrp", bufs=FRONT_BUFS, align_bytes=64)
             nc.vector.tensor_copy(
                 out=g[:].rearrange("p (c i) t -> p c t i", i=4),
-                in_=st[("wide", c)][:].rearrange("p t (c i) -> p c t i", i=4),
+                in_=st[("wide", u)][:].rearrange("p t (c i) -> p c t i", i=4),
             )
-            st[("whgrp", c)] = g
+            st[("whgrp", u)] = g
 
-        def wh_q(c):
-            quant("w", c, st[("whgrp", c)], CHUNKS[c][2])
+        def wh_q(u):
+            quant("w", u, st[("whgrp", u)], LOADS[u][2])
 
-        def product(nm, wn, c, tag, j):
+        def product(nm, wn, c, j):
             n = CHUNKS[c][2]
-            codes, scs = st[(nm, c)]
-            ps = psum.tile([P, n], F32, name="ps_%s_%d_%d" % (nm, c, j), tag=tag, bufs=A_BUFS if tag == "a" else O_BUFS)
+            u, off = (c, 0) if nm == "h" else units[c]
+            codes, scs = st[(nm, u)]
+            ps = psum.tile([P, n], F32, name="ps_%s_%d_%d" % (nm, c, j), tag="a", bufs=A_BUFS)
             cols = slice(P * j, P * (j + 1))
             nc.tensor.matmul_mx(
                 out=ps[:], lhsT=w_codes[wn][:, cols].bitcast(FP8X4), lhsT_scale=w_scales[wn][:, cols],
-                rhs=codes[:].bitcast(FP8X4), rhs_scale=scs[:], start=True, stop=True,
+                rhs=codes[:, off : off + n].bitcast(FP8X4), rhs_scale=scs[:, off : off + n], start=True, stop=True,
             )
             st[("ps" + nm, c, j)] = ps
 
         def gate_in(nm, wn, c):
             for j in range(J):
-                product(nm, wn, c, "a", j)
+                product(nm, wn, c, j)
 
         def tanh_in(nm, wn, c):
             n = CHUNKS[c][2]
             if ("t", c) not in st:
-                st[("t", c)] = work.tile([P, 2, J, n], F32, name="t_%d" % c, tag="t", align_bytes=64)
+                st[("t", c)] = work.tile([P, 2, J, n], F32, name="t_%d" % c, tag="t", bufs=2, align_bytes=64)
             t = st[("t", c)]
             k = 0 if nm == "g" else 1
             for j in range(J):
                 nc.scalar.activation(out=t[:, k, j, :], in_=st[("ps" + nm, c, j)][:], func=ACT.Tanh, bias=bias[wn][:, j : j + 1])
 
         def tanh_out(c, lo, hi):
-            if lo == hi:
-                return
             part = st[("t", c)][:, :, :, lo:hi]
             nc.scalar.activation(out=part, in_=part, func=ACT.Tanh, scale=0.5)
 
         def split(c):
-            n = CHUNKS[c][2]
-            return n, PE_SLABS[n] * SLAB
+            return CHUNKS[c][2], SLAB if c in PE_CHUNKS else 0
 
         def pe_sum(c):
-            n, m = split(c)
-            for lo in range(0, m, SLAB):
-                ps = psum.tile([P, J, SLAB], F32, name="gs_%d_%d" % (c, lo), tag="s", bufs=S_BUFS)
-                for k in range(2):
-                    nc.tensor.matmul(out=ps[:], lhsT=ident[:], rhs=st[("t", c)][:, k, :, lo : lo + SLAB], start=(k == 0), stop=(k == 1))
-                st[("gs", c, lo)] = ps
+            ps = psum.tile([P, J, SLAB], F32, name="gs_%d" % c, tag="a", bufs=A_BUFS)
+            for k in range(2):
+                nc.tensor.matmul(out=ps[:], lhsT=ident[:], rhs=st[("t", c)][:, k, :, :SLAB], start=(k == 0), stop=(k == 1))
+            st[("gs", c)] = ps
 
         def get_h(c):
             if ("hgrp", c) not in st:
@@ -219,27 +219,21 @@ def tile_wb_pb_t_kernel(tc, x, wh_bytes, wh_scale, gray, W2, b2, W3, b3, W4, b4,
             return st[("hgrp", c)]
 
         def pe_mul(c):
-            n, m = split(c)
             xt, off, n = find("x", c)
-            h = get_h(c)
-            for lo in range(0, m, SLAB):
-                nc.vector.scalar_tensor_tensor(
-                    out=h[:, lo : lo + SLAB, :], in0=st[("gs", c, lo)][:].rearrange("p t n -> p n t"), scalar=4.0,
-                    in1=xt[:, :, off + lo : off + lo + SLAB].rearrange("p t n -> p n t"), op0=ALU.add, op1=ALU.mult,
-                )
+            nc.vector.scalar_tensor_tensor(
+                out=get_h(c)[:, :SLAB, :].rearrange("p (c i) t -> p c t i", i=4),
+                in0=st[("gs", c)][:].rearrange("p t (c i) -> p c t i", i=4), scalar=4.0,
+                in1=xt[:, :, off : off + SLAB].rearrange("p t (c i) -> p c t i", i=4), op0=ALU.add, op1=ALU.mult,
+            )
 
         def gate_sum(c):
             n, m = split(c)
-            if m == n:
-                return
             t = st[("t", c)]
             nc.vector.scalar_tensor_tensor(
                 out=t[:, 0, :, m:n], in0=t[:, 1, :, m:n], scalar=4.0, in1=t[:, 0, :, m:n], op0=ALU.add, op1=ALU.add)
 
         def gate_mul(c):
             n, m = split(c)
-            if m == n:
-                return
             xt, off, n = find("x", c)
             h = get_h(c)
             nc.vector.tensor_tensor(
@@ -252,89 +246,80 @@ def tile_wb_pb_t_kernel(tc, x, wh_bytes, wh_scale, gray, W2, b2, W3, b3, W4, b4,
         def h_q(c):
             quant("h", c, st[("hgrp", c)], CHUNKS[c][2])
 
-        def conv_out(c):
-            n = CHUNKS[c][2]
-            for j in range(J):
-                product("h", "4", c, "o", j)
-            st[("o", c)] = work.tile([P, J, n], F32, name="o_%d" % c, tag="o", align_bytes=64)
+        def conv_out(c, js):
+            for j in js:
+                product("h", "4", c, j)
 
-        def empty_v(c):
-            for j in OUT_ON_VECTOR[c]:
-                nc.vector.tensor_scalar(
-                    out=st[("o", c)][:, j, :], in0=st[("psh", c, j)][:], scalar1=0.5, scalar2=bias["4"][:, j : j + 1],
-                    op0=ALU.mult, op1=ALU.add,
-                )
+        def get_o(c):
+            if ("o", c) not in st:
+                st[("o", c)] = work.tile([P, J, CHUNKS[c][2]], F32, name="o_%d" % c, tag="o", bufs=3, align_bytes=64)
+            return st[("o", c)]
 
-        def empty_s(c):
-            for j in range(J):
-                if j not in OUT_ON_VECTOR[c]:
-                    nc.scalar.activation(
-                        out=st[("o", c)][:, j, :], in_=st[("psh", c, j)][:], func=ACT.Identity, scale=0.5, bias=bias["4"][:, j : j + 1],
-                    )
+        def empty(c, j, eng):
+            o = get_o(c)[:, j, :]
+            ps = st[("psh", c, j)]
+            if eng == "v":
+                nc.vector.tensor_scalar(out=o, in0=ps[:], scalar1=0.5, scalar2=bias["4"][:, j : j + 1], op0=ALU.mult, op1=ALU.add)
+            else:
+                nc.scalar.activation(out=o, in_=ps[:], func=ACT.Identity, scale=0.5, bias=bias["4"][:, j : j + 1])
 
-        def store(c):
+        def store(c, j0, j1):
             b, c0, n = CHUNKS[c]
             v = out[b].rearrange("(p t) h w -> p t (h w)", t=J)
-            step = 2 if c >= n_chunks - SPLIT_STORES else J
-            for j in range(0, J, step):
-                nc.sync.dma_start(out=v[:, j : j + step, c0 : c0 + n], in_=st[("o", c)][:, j : j + step, :])
+            nc.sync.dma_start(out=v[:, j0:j1, c0 : c0 + n], in_=st[("o", c)][:, j0:j1, :])
 
-        def emit(task, c):
+        def emit(task, a):
             if task == "wt":
-                w_transpose(c[0], int(c[1]))
+                w_transpose(a[0], int(a[1]))
             elif task in ("wcs", "wcv"):
-                w_copy(c[0], int(c[1]), task[2])
+                w_copy(a[0], int(a[1]), task[2])
             elif task == "wqz":
-                if c[1] == "0":
-                    bias_cast(c[0])
-                w_quant(c[0], int(c[1]))
-            elif task == "gil":
-                gray_il(c)
-            elif task == "gq":
-                gray_q(c)
-            elif task == "ww":
-                wh_widen(c)
-            elif task == "wil":
-                wh_il(c)
-            elif task == "wq":
-                wh_q(c)
-            elif task == "m1g":
-                gate_in("g", "3", c)
-            elif task == "m1w":
-                gate_in("w", "2", c)
-            elif task == "t1g":
-                tanh_in("g", "3", c)
-            elif task == "t1w":
-                tanh_in("w", "2", c)
-            elif task == "t2a":
-                tanh_out(c, 0, split(c)[1])
-            elif task == "t2b":
-                tanh_out(c, *split(c)[::-1])
-            elif task == "psum":
-                pe_sum(c)
-            elif task == "mulp":
-                pe_mul(c)
-            elif task == "sum":
-                gate_sum(c)
-            elif task == "mul":
-                gate_mul(c)
-            elif task == "hq":
-                h_q(c)
-            elif task == "m2":
-                conv_out(c)
-            elif task == "ev":
-                empty_v(c)
-            elif task == "es":
-                empty_s(c)
-                store(c)
+                if a[1] == "0":
+                    bias_cast(a[0])
+                w_quant(a[0], int(a[1]))
+            else:
+                n = [int(v) for v in a.split(".")]
+                c = n[0]
+                if task in ("giv", "gis"):
+                    gray_il(c, task[2])
+                elif task == "gq":
+                    gray_q(c)
+                elif task in ("wwv", "wws"):
+                    wh_widen(c, task[2])
+                elif task == "wil":
+                    wh_il(c)
+                elif task == "wq":
+                    wh_q(c)
+                elif task == "mg":
+                    gate_in("g", "3", c)
+                elif task == "mw":
+                    gate_in("w", "2", c)
+                elif task == "tg":
+                    tanh_in("g", "3", c)
+                elif task == "tw":
+                    tanh_in("w", "2", c)
+                elif task == "ua":
+                    tanh_out(c, 0, split(c)[1])
+                elif task == "ub":
+                    tanh_out(c, *split(c)[::-1])
+                elif task == "ps":
+                    pe_sum(c)
+                elif task == "pm":
+                    pe_mul(c)
+                elif task == "sum":
+                    gate_sum(c)
+                elif task == "mul":
+                    gate_mul(c)
+                elif task == "hq":
+                    h_q(c)
+                elif task == "ma":
+                    conv_out(c, (0, 1))
+                elif task == "mb":
+                    conv_out(c, (2, 3))
+                elif task in ("ev", "es"):
+                    empty(c, n[1], task[1])
+                elif task == "st":
+                    store(c, n[1], n[2])
 
-        done = set()
-        for task, c in HEAD:
-            emit(task, c)
-            done.add((task, c))
-        for i in range(-3, n_chunks + 4):
-            for task, off in ORDER:
-                c = i + off
-                if 0 <= c < n_chunks and (task, c) not in done:
-                    emit(task, c)
-                    done.add((task, c))
+        for item in SEQ.split():
+            emit(*item.split(":"))

from contextlib import ExitStack

import concourse.mybir as mybir
from concourse.masks import make_identity

B, C, P_IMG = 4, 512, 1024
P = 128
J = 4
FLOPS = 3 * 2 * B * C * C * P_IMG

F32 = mybir.dt.float32
BF16 = mybir.dt.bfloat16
U32 = mybir.dt.uint32
U8 = mybir.dt.uint8
FP8 = mybir.dt.float8_e4m3fn
FP8X4 = mybir.dt.float8_e4m3fn_x4
ALU = mybir.AluOpType
ACT = mybir.ActivationFunctionType

LOADS = [(0, 0, 256), (0, 256, 256), (0, 512, 512), (1, 0, 1024), (2, 0, 1024), (3, 0, 1024)]
LOAD_ORDER = "w0 w1 W20 W21 w2 g0 W30 W31 g1 w3 g2 W40 x0 W41 g4 g3 x1 g5 w5 x4 w4 x3 x2 x5"
CHUNKS = [(0, 0, 256), (0, 256, 256), (0, 512, 512), (1, 0, 512), (1, 512, 512), (2, 0, 512), (2, 512, 512), (3, 0, 512), (3, 512, 256), (3, 768, 256)]
A_BUFS = 8
SLAB = 128
FRONT_BUFS = 1
PE_CHUNKS = ()
SEQ = "wt:20 wws:1 wcs:20 wt:21 wwv:0 wil:0 wq:0 wil:1 wqz:20 wcs:21 wq:1 wqz:21 gis:0 mw:0 wt:30 wwv:2 gq:0 wt:31 tw:0 wil:2 giv:1 wcs:30 wcs:31 wqz:30 wqz:31 gq:1 mw:1 tw:1 mg:0 tg:0 wwv:3 giv:2 wq:2 ub:0 sum:0 gq:2 mul:0 mg:1 wt:40 wil:3 tg:1 giv:3 wcs:40 mg:2 wq:3 mw:2 ub:1 tg:2 hq:0 tw:2 wt:41 gq:3 sum:1 mw:3 wqz:40 mul:1 wcs:41 ma:0 ub:2 wqz:41 tw:3 mb:0 giv:4 mg:3 es:0.3 sum:2 hq:1 tg:3 ev:0.0 mul:2 ev:0.1 es:0.2 wwv:4 mw:4 hq:2 ub:3 gq:4 tw:4 sum:3 wil:4 ma:2 mg:4 mb:2 ev:2.2 es:2.1 tg:4 st:0.0.4 es:2.3 mul:3 wq:4 es:2.0 giv:5 ub:4 sum:4 mg:5 mb:1 gq:5 tg:5 mw:5 tw:5 ma:1 hq:3 es:1.2 mul:4 es:1.1 ub:5 ev:1.3 wwv:5 mg:6 tg:6 hq:4 ev:1.0 mw:6 tw:6 mb:4 sum:5 st:2.0.4 es:4.3 wil:5 mg:7 mul:5 ev:4.2 ub:6 wq:5 mb:3 tg:7 mw:7 tw:7 sum:6 es:3.2 ev:3.3 ma:3 ev:3.0 ma:4 mul:6 ub:7 mw:8 ev:3.1 ev:4.0 tw:8 hq:5 ma:5 st:1.0.4 st:3.0.4 ev:4.1 st:4.0.4 mg:8 hq:6 tg:8 es:5.1 mb:5 sum:7 es:5.0 ev:5.2 mw:9 mul:7 ma:6 ub:8 tw:9 ev:5.3 ev:6.0 ev:6.1 mg:9 hq:7 mb:6 sum:8 mb:7 ev:6.3 tg:9 es:6.2 ma:7 ub:9 ev:7.2 ev:7.0 mul:8 sum:9 hq:8 st:5.0.4 mb:8 es:7.3 es:7.1 es:8.2 ma:8 mul:9 ev:8.0 es:8.3 hq:9 st:6.0.4 es:8.1 st:7.0.4 ma:9 mb:9 es:9.0 es:9.3 ev:9.1 st:8.0.4 st:9.0.2 ev:9.2 st:9.2.4"


def tile_wb_pb_t_kernel(tc, x, wh_bytes, wh_scale, gray, W2, b2, W3, b3, W4, b4, out):
    nc = tc.nc
    n_chunks = len(CHUNKS)

    with ExitStack() as ctx:
        keep = ctx.enter_context(tc.tile_pool(name="keep", bufs=1))
        work = ctx.enter_context(tc.tile_pool(name="work", bufs=2))
        psum = ctx.enter_context(tc.psum_pool(name="psum", bufs=8))

        ident = keep.tile([P, P], F32, name="ident", align_bytes=64)
        make_identity(nc, ident[:])
        ctx.enter_context(tc.manual_schedule())

        warm = keep.tile([P, 1], F32, name="warm")
        nc.vector.memset(warm[:], 0.0)
        nc.scalar.activation(out=warm[:], in_=warm[:], func=ACT.Tanh)

        w_rows = {}
        bias_b = {}
        imgs = {}

        def load_w(nm, w, h):
            if nm not in w_rows:
                w_rows[nm] = keep.tile([P, J, C], BF16, name="wrows_" + nm, align_bytes=64)
            src = w.rearrange("(m t) k -> m t k", t=J)
            nc.sync.dma_start(out=w_rows[nm][:, 2 * h : 2 * h + 2, :], in_=src[:, 2 * h : 2 * h + 2, :])

        def load_bias(nm, b):
            t = keep.tile([P, J], BF16, name="biasb_" + nm)
            nc.scalar.dma_start(out=t[:], in_=b.rearrange("(p t) -> p t", t=J))
            bias_b[nm] = t

        def load_img(nm, src, u, dt):
            b, c0, n = LOADS[u]
            t = keep.tile([P, J, n], dt, name="%s_%d" % (nm, u), align_bytes=64)
            v = src[b].rearrange("(p t) h w -> p t (h w)", t=J)
            nc.sync.dma_start(out=t[:], in_=v[:, :, c0 : c0 + n])
            imgs[(nm, u)] = t

        def find(nm, c):
            b, c0, n = CHUNKS[c]
            for u in range(len(LOADS)):
                lb, l0, ln = LOADS[u]
                if lb == b and l0 <= c0 and c0 + n <= l0 + ln:
                    return imgs[(nm, u)], c0 - l0, n
            return None

        scale = keep.tile([P, J], F32, name="scale")
        nc.scalar.dma_start(out=scale[:], in_=wh_scale.rearrange("o (p t) a b -> p (o t a b)", t=J))
        load_bias("3", b3)
        load_bias("2", b2)
        load_bias("4", b4)
        srcs = {"g": ("gray", gray, BF16), "w": ("wh", wh_bytes, U8), "x": ("x", x, BF16)}
        for item in LOAD_ORDER.split():
            if item[0] == "W":
                load_w(item[1], {"2": W2, "3": W3, "4": W4}[item[1]], int(item[2]))
            else:
                nm, src, dt = srcs[item[0]]
                load_img(nm, src, int(item[1:]), dt)

        w_codes, w_scales, w_grp, w_ps = {}, {}, {}, {}

        def w_transpose(nm, h):
            ps = psum.tile([P, 2, 2, P], F32, name="wps_%s%d" % (nm, h), tag="a", bufs=A_BUFS)
            for s in range(2):
                words = w_rows[nm][:, 2 * h + s, :].bitcast(F32)
                for u in range(2):
                    nc.tensor.transpose(ps[:, s, u, :], words[:, u : C // 2 : 2], ident[:])
            w_ps[(nm, h)] = ps
            if nm not in w_grp:
                w_grp[nm] = keep.tile([P, C * J], BF16, name="wgrp_" + nm, align_bytes=64)

        def w_copy(nm, h, eng):
            dst = w_grp[nm][:].bitcast(F32).rearrange("p (h s m u) -> p h s m u", h=2, s=2, u=2)[:, h]
            src = w_ps[(nm, h)][:].rearrange("p s u m -> p s m u")
            if eng == "v":
                nc.vector.tensor_copy(out=dst, in_=src)
            else:
                nc.scalar.copy(out=dst, in_=src)

        def w_quant(nm, h):
            if nm not in w_codes:
                w_codes[nm] = keep.tile([P, C], U32, name="wcodes_" + nm, align_bytes=64)
                w_scales[nm] = keep.tile([P, C], U8, name="wscales_" + nm, align_bytes=64)
            cols = slice(C // 2 * h, C // 2 * (h + 1))
            nc.vector.quantize_mx(
                out=w_codes[nm][:, cols].bitcast(FP8X4), scales=w_scales[nm][:, cols],
                in_=w_grp[nm][:, C // 2 * J * h : C // 2 * J * (h + 1)])

        bias = {}

        def bias_cast(nm):
            bias[nm] = keep.tile([P, J], F32, name="bias_" + nm)
            nc.vector.tensor_copy(out=bias[nm][:], in_=bias_b[nm][:])

        st = {}

        units = {}
        for c in range(n_chunks):
            b, c0, n = CHUNKS[c]
            for u in range(len(LOADS)):
                lb, l0, ln = LOADS[u]
                if lb == b and l0 <= c0 and c0 + n <= l0 + ln:
                    units[c] = (u, c0 - l0)

        def quant(nm, c, grp, n):
            codes = work.tile([P, n], U32, name="codes_%s_%d" % (nm, c), tag="codes_" + nm, align_bytes=64)
            scs = work.tile([P, n], U8, name="scs_%s_%d" % (nm, c), tag="scs_" + nm, align_bytes=64)
            nc.vector.quantize_mx(out=codes[:].bitcast(FP8X4), scales=scs[:], in_=grp[:].rearrange("p n t -> p (n t)"))
            st[(nm, c)] = (codes, scs)

        def gray_il(u, eng):
            n = LOADS[u][2]
            g = st.get(("ggrp", u)) or work.tile([P, n, J], BF16, name="ggrp_%d" % u, tag="ggrp", bufs=FRONT_BUFS, align_bytes=64)
            dst = g[:].rearrange("p (c i) t -> p c t i", i=4)
            src = imgs[("gray", u)][:].rearrange("p t (c i) -> p c t i", i=4)
            if eng == "v":
                nc.vector.tensor_copy(out=dst, in_=src)
            else:
                nc.scalar.copy(out=dst, in_=src)
            st[("ggrp", u)] = g

        def gray_q(u):
            quant("g", u, st[("ggrp", u)], LOADS[u][2])

        def wh_widen(u, eng):
            n = LOADS[u][2]
            wd = st.get(("wide", u)) or work.tile([P, J, n], BF16, name="wide_%d" % u, tag="wide", bufs=2, align_bytes=64)
            for j in range(J):
                codes = imgs[("wh", u)][:, j, :].bitcast(FP8)
                if eng == "v":
                    nc.vector.tensor_scalar(out=wd[:, j, :], in0=codes, scalar1=scale[:, j : j + 1], scalar2=None, op0=ALU.mult)
                else:
                    nc.scalar.activation(out=wd[:, j, :], in_=codes, func=ACT.Copy, scale=scale[:, j : j + 1])
            st[("wide", u)] = wd

        def wh_il(u):
            n = LOADS[u][2]
            g = work.tile([P, n, J], BF16, name="wgrp_%d" % u, tag="wgrp", bufs=FRONT_BUFS, align_bytes=64)
            nc.vector.tensor_copy(
                out=g[:].rearrange("p (c i) t -> p c t i", i=4),
                in_=st[("wide", u)][:].rearrange("p t (c i) -> p c t i", i=4),
            )
            st[("whgrp", u)] = g

        def wh_q(u):
            quant("w", u, st[("whgrp", u)], LOADS[u][2])

        def product(nm, wn, c, j):
            n = CHUNKS[c][2]
            u, off = (c, 0) if nm == "h" else units[c]
            codes, scs = st[(nm, u)]
            ps = psum.tile([P, n], F32, name="ps_%s_%d_%d" % (nm, c, j), tag="a", bufs=A_BUFS)
            cols = slice(P * j, P * (j + 1))
            nc.tensor.matmul_mx(
                out=ps[:], lhsT=w_codes[wn][:, cols].bitcast(FP8X4), lhsT_scale=w_scales[wn][:, cols],
                rhs=codes[:, off : off + n].bitcast(FP8X4), rhs_scale=scs[:, off : off + n], start=True, stop=True,
            )
            st[("ps" + nm, c, j)] = ps

        def gate_in(nm, wn, c):
            for j in range(J):
                product(nm, wn, c, j)

        def tanh_in(nm, wn, c):
            n = CHUNKS[c][2]
            if ("t", c) not in st:
                st[("t", c)] = work.tile([P, 2, J, n], F32, name="t_%d" % c, tag="t", bufs=2, align_bytes=64)
            t = st[("t", c)]
            k = 0 if nm == "g" else 1
            for j in range(J):
                nc.scalar.activation(out=t[:, k, j, :], in_=st[("ps" + nm, c, j)][:], func=ACT.Tanh, bias=bias[wn][:, j : j + 1])

        def tanh_out(c, lo, hi):
            part = st[("t", c)][:, :, :, lo:hi]
            nc.scalar.activation(out=part, in_=part, func=ACT.Tanh, scale=0.5)

        def split(c):
            return CHUNKS[c][2], SLAB if c in PE_CHUNKS else 0

        def pe_sum(c):
            ps = psum.tile([P, J, SLAB], F32, name="gs_%d" % c, tag="a", bufs=A_BUFS)
            for k in range(2):
                nc.tensor.matmul(out=ps[:], lhsT=ident[:], rhs=st[("t", c)][:, k, :, :SLAB], start=(k == 0), stop=(k == 1))
            st[("gs", c)] = ps

        def get_h(c):
            if ("hgrp", c) not in st:
                st[("hgrp", c)] = work.tile([P, CHUNKS[c][2], J], BF16, name="h_%d" % c, tag="h", align_bytes=64)
            return st[("hgrp", c)]

        def pe_mul(c):
            xt, off, n = find("x", c)
            nc.vector.scalar_tensor_tensor(
                out=get_h(c)[:, :SLAB, :].rearrange("p (c i) t -> p c t i", i=4),
                in0=st[("gs", c)][:].rearrange("p t (c i) -> p c t i", i=4), scalar=4.0,
                in1=xt[:, :, off : off + SLAB].rearrange("p t (c i) -> p c t i", i=4), op0=ALU.add, op1=ALU.mult,
            )

        def gate_sum(c):
            n, m = split(c)
            t = st[("t", c)]
            nc.vector.scalar_tensor_tensor(
                out=t[:, 0, :, m:n], in0=t[:, 1, :, m:n], scalar=4.0, in1=t[:, 0, :, m:n], op0=ALU.add, op1=ALU.add)

        def gate_mul(c):
            n, m = split(c)
            xt, off, n = find("x", c)
            h = get_h(c)
            nc.vector.tensor_tensor(
                out=h[:, m:n, :].rearrange("p (c i) t -> p c t i", i=4),
                in0=st[("t", c)][:, 0, :, m:n].rearrange("p t (c i) -> p c t i", i=4),
                in1=xt[:, :, off + m : off + n].rearrange("p t (c i) -> p c t i", i=4),
                op=ALU.mult,
            )

        def h_q(c):
            quant("h", c, st[("hgrp", c)], CHUNKS[c][2])

        def conv_out(c, js):
            for j in js:
                product("h", "4", c, j)

        def get_o(c):
            if ("o", c) not in st:
                st[("o", c)] = work.tile([P, J, CHUNKS[c][2]], F32, name="o_%d" % c, tag="o", bufs=3, align_bytes=64)
            return st[("o", c)]

        def empty(c, j, eng):
            o = get_o(c)[:, j, :]
            ps = st[("psh", c, j)]
            if eng == "v":
                nc.vector.tensor_scalar(out=o, in0=ps[:], scalar1=0.5, scalar2=bias["4"][:, j : j + 1], op0=ALU.mult, op1=ALU.add)
            else:
                nc.scalar.activation(out=o, in_=ps[:], func=ACT.Identity, scale=0.5, bias=bias["4"][:, j : j + 1])

        def store(c, j0, j1):
            b, c0, n = CHUNKS[c]
            v = out[b].rearrange("(p t) h w -> p t (h w)", t=J)
            nc.sync.dma_start(out=v[:, j0:j1, c0 : c0 + n], in_=st[("o", c)][:, j0:j1, :])

        def emit(task, a):
            if task == "wt":
                w_transpose(a[0], int(a[1]))
            elif task in ("wcs", "wcv"):
                w_copy(a[0], int(a[1]), task[2])
            elif task == "wqz":
                if a[1] == "0":
                    bias_cast(a[0])
                w_quant(a[0], int(a[1]))
            else:
                n = [int(v) for v in a.split(".")]
                c = n[0]
                if task in ("giv", "gis"):
                    gray_il(c, task[2])
                elif task == "gq":
                    gray_q(c)
                elif task in ("wwv", "wws"):
                    wh_widen(c, task[2])
                elif task == "wil":
                    wh_il(c)
                elif task == "wq":
                    wh_q(c)
                elif task == "mg":
                    gate_in("g", "3", c)
                elif task == "mw":
                    gate_in("w", "2", c)
                elif task == "tg":
                    tanh_in("g", "3", c)
                elif task == "tw":
                    tanh_in("w", "2", c)
                elif task == "ua":
                    tanh_out(c, 0, split(c)[1])
                elif task == "ub":
                    tanh_out(c, *split(c)[::-1])
                elif task == "ps":
                    pe_sum(c)
                elif task == "pm":
                    pe_mul(c)
                elif task == "sum":
                    gate_sum(c)
                elif task == "mul":
                    gate_mul(c)
                elif task == "hq":
                    h_q(c)
                elif task == "ma":
                    conv_out(c, (0, 1))
                elif task == "mb":
                    conv_out(c, (2, 3))
                elif task in ("ev", "es"):
                    empty(c, n[1], task[1])
                elif task == "st":
                    store(c, n[1], n[2])

        for item in SEQ.split():
            emit(*item.split(":"))
